import numpy as np
import ml_dtypes


def mxq(x, axis, fmt="e4m3"):
    dtype, down = {"e4m3": (ml_dtypes.float8_e4m3fn, 7), "e5m2": (ml_dtypes.float8_e5m2, 14)}[fmt]
    v = np.moveaxis(np.asarray(x, np.float32).astype(ml_dtypes.bfloat16).astype(np.float64), axis, -1)
    blocks = v.reshape(v.shape[:-1] + (-1, 32))
    amax = np.abs(blocks).max(-1, keepdims=True)
    byte = np.maximum(np.where(amax > 0, np.frexp(amax)[1] - 1 + 127, 0) - down, 1)
    scale = np.exp2(byte - 127.0)
    codes = (blocks / scale).astype(np.float32).astype(dtype).astype(np.float64)
    return np.moveaxis((codes * scale).reshape(v.shape), -1, axis)


WIDE = False


def mx_kscale(k):
    if not WIDE:
        return np.ones(k)
    levels = np.array([10, -10, 5, -5, 0])
    a = np.random.permutation(np.resize(levels, k // 512 * 4)).reshape(k // 512, 4)
    idx = np.arange(k)
    return np.exp2(a[idx // 512, idx % 128 // 32])


BF16 = ml_dtypes.bfloat16


def bf(x):
    return np.asarray(x, np.float32).astype(BF16)


def f64(x):
    return np.asarray(x).astype(np.float64)


B, S, H, A, NH = 4, 128, 1536, 1536, 12
HD = A // NH
LN_EPS = 1e-5


def setup_inputs():
    s = mx_kscale(A)
    return {"ctx_heads": bf(np.random.standard_normal((B, NH, S, HD)) * s.reshape(NH, 1, HD)),
            "Wo": bf(np.random.standard_normal((H, A)) / np.sqrt(A) / s),
            "bo": bf(np.random.standard_normal(H) * 0.3),
            "features": bf(np.random.standard_normal((B, S, H))),
            "ln_g": bf(1.0 + 0.1 * np.random.standard_normal(H)),
            "ln_b": bf(0.2 * np.random.standard_normal(H))}


def reference(ctx_heads, Wo, bo, features, ln_g, ln_b):
    ctx = f64(ctx_heads).transpose(0, 2, 1, 3).reshape(B, S, A)
    p = (mxq(ctx, 2, "e4m3") @ mxq(f64(Wo), 1, "e4m3").T) + f64(bo)
    y = p + f64(features)
    mu = y.mean(-1, keepdims=True)
    var = y.var(-1, keepdims=True)
    return (y - mu) / np.sqrt(var + LN_EPS) * f64(ln_g) + f64(ln_b)

@@ -1,0 +1,171 @@
+from contextlib import ExitStack
+
+import concourse.mybir as mybir
+from concourse.masks import make_identity
+
+FP8X4 = mybir.dt.float8_e4m3fn_x4
+BF16 = mybir.dt.bfloat16
+F32 = mybir.dt.float32
+I32 = mybir.dt.int32
+U32 = mybir.dt.uint32
+U8 = mybir.dt.uint8
+ADD = mybir.AluOpType.add
+MULT = mybir.AluOpType.mult
+ACT = mybir.ActivationFunctionType
+
+P = 128
+BATCH = 4
+HEADS = 12
+K = 1536
+H = 1536
+LN_EPS = 1e-5
+
+PACK = 4
+K_PASS = P * PACK
+PASSES = K // K_PASS
+WORDS_PASS = K_PASS // 2
+ROWS = 512
+BLOCKS = ROWS // P
+N_TILES = H // ROWS
+
+FLOPS = 2 * BATCH * P * K * H
+
+
+def quantise_rows(nc, psum_t, stage, ident, sources, codes, scales):
+    for g in range(PASSES):
+        grouped = stage.tile([P, ROWS * PACK], BF16, name="grouped", align_bytes=64)
+        grouped_words = grouped[:].bitcast(F32).rearrange("p (i r u) -> p i r u", i=BLOCKS, u=2)
+        for pair in range(BLOCKS // 2):
+            bank = psum_t.tile([P, 2, 2, P], F32, name="bank")
+            for i in range(2):
+                words = sources[2 * pair + i][:].bitcast(F32)
+                for u in range(2):
+                    first = WORDS_PASS * g + P * u
+                    nc.tensor.transpose(bank[:, i, u, :], words[:, first : first + P], ident[:])
+            nc.scalar.copy(
+                out=grouped_words[:, 2 * pair : 2 * pair + 2, :, :],
+                in_=bank[:].rearrange("p i u r -> p i r u"),
+            )
+        nc.vector.quantize_mx(out=codes[:, g, :].bitcast(FP8X4), scales=scales[:, g, :], in_=grouped[:])
+
+
+def tile_hierarchicalattention_pb_kernel(tc, ctx_heads, Wo, bo, features, ln_g, ln_b, out):
+    nc = tc.nc
+    with ExitStack() as stack:
+        const = stack.enter_context(tc.tile_pool(name="const", bufs=1))
+        loads = stack.enter_context(tc.tile_pool(name="loads", bufs=1))
+        stage = stack.enter_context(tc.tile_pool(name="stage", bufs=4))
+        keep = stack.enter_context(tc.tile_pool(name="keep", bufs=1))
+        junk_pool = stack.enter_context(tc.tile_pool(name="junk", bufs=2))
+        psum_t = stack.enter_context(tc.psum_pool(name="psum_t", bufs=4))
+        psum_acc = stack.enter_context(tc.psum_pool(name="psum_acc", bufs=4))
+
+        ident = const.tile([P, P], F32, name="ident")
+        make_identity(nc, ident[:])
+        ones = const.tile([P, P], BF16, name="ones")
+        nc.vector.memset(ones[:], 1.0)
+        vec_rows = const.tile([P, 3 * H], BF16, name="vec_rows")
+        nc.vector.memset(vec_rows[:].bitcast(I32), 0)
+        one_col = const.tile([P, 1], F32, name="one_col")
+        nc.vector.memset(one_col[:], 1.0)
+        warm = const.tile([P, 1], F32, name="warm")
+        nc.scalar.activation(out=warm[:], in_=one_col[:], func=ACT.Sqrt)
+
+        for v, vec in enumerate((bo, ln_g, ln_b)):
+            nc.sync.dma_start(out=vec_rows[0:1, v * H : (v + 1) * H], in_=vec.rearrange("(o n) -> o n", o=1))
+        ctx_sb = []
+        for b in range(BATCH):
+            t = loads.tile([P, K], BF16, name="ctx_sb%d" % b)
+            nc.sync.dma_start(
+                out=t[:].rearrange("s (h d) -> s h d", h=HEADS), in_=ctx_heads[b].rearrange("h s d -> s h d")
+            )
+            ctx_sb.append(t)
+        wo_sb = []
+        f_sb = []
+        for r in range(H // P):
+            t = loads.tile([P, K], BF16, name="wo_sb%d" % r)
+            nc.sync.dma_start(out=t[:], in_=Wo[r * P : (r + 1) * P, :])
+            wo_sb.append(t)
+            if r == BLOCKS - 1:
+                for b in range(BATCH):
+                    f = loads.tile([P, H], BF16, name="f_sb%d" % b)
+                    nc.sync.dma_start(out=f[:], in_=features[b])
+                    f_sb.append(f)
+
+        spread = []
+        for v in range(3):
+            s = const.tile([P, H], BF16, name="spread%d" % v)
+            for j in range(N_TILES):
+                ps = psum_acc.tile([P, ROWS], F32, name="acc")
+                first = v * H + j * ROWS
+                nc.tensor.matmul(out=ps[:], lhsT=ones[:], rhs=vec_rows[:, first : first + ROWS], start=True, stop=True)
+                nc.vector.tensor_copy(out=s[:, j * ROWS : (j + 1) * ROWS], in_=ps[:])
+            spread.append(s)
+        bo_all, g_all, b_all = spread
+
+        ctx_codes = keep.tile([P, PASSES, ROWS], U32, name="ctx_codes", align_bytes=64)
+        ctx_scales = keep.tile([P, PASSES, ROWS], U8, name="ctx_scales", align_bytes=64)
+        quantise_rows(nc, psum_t, stage, ident, ctx_sb, ctx_codes, ctx_scales)
+
+        y = []
+        rowsum = []
+        for b in range(BATCH):
+            y.append(keep.tile([P, H], F32, name="y%d" % b))
+            rowsum.append(keep.tile([P, N_TILES], F32, name="rowsum%d" % b))
+        for j in range(N_TILES):
+            wo_codes = keep.tile([P, PASSES, ROWS], U32, name="wo_codes%d" % j, align_bytes=64)
+            wo_scales = keep.tile([P, PASSES, ROWS], U8, name="wo_scales%d" % j, align_bytes=64)
+            quantise_rows(nc, psum_t, stage, ident, wo_sb[j * BLOCKS : (j + 1) * BLOCKS], wo_codes, wo_scales)
+            if j == 0:
+                for b in range(BATCH):
+                    nc.vector.tensor_tensor(out=y[b][:], in0=f_sb[b][:], in1=bo_all[:], op=ADD)
+            cols = slice(j * ROWS, (j + 1) * ROWS)
+            for b in range(BATCH):
+                tokens = slice(b * P, (b + 1) * P)
+                acc = psum_acc.tile([P, ROWS], F32, name="acc")
+                for g in range(PASSES):
+                    nc.tensor.matmul_mx(
+                        out=acc[:],
+                        lhsT=ctx_codes[:, g, tokens].bitcast(FP8X4),
+                        lhsT_scale=ctx_scales[:, g, tokens],
+                        rhs=wo_codes[:, g, :].bitcast(FP8X4),
+                        rhs_scale=wo_scales[:, g, :],
+                        start=(g == 0),
+                        stop=(g == PASSES - 1),
+                    )
+                nc.vector.scalar_tensor_tensor(
+                    out=y[b][:, cols],
+                    in0=acc[:],
+                    scalar=1.0,
+                    in1=y[b][:, cols],
+                    op0=MULT,
+                    op1=ADD,
+                    accum_out=rowsum[b][:, j : j + 1],
+                )
+
+        negmean = []
+        sumsq = []
+        for b in range(BATCH + 1):
+            if b < BATCH:
+                total = keep.tile([P, 1], F32, name="total%d" % b)
+                nc.vector.tensor_reduce(out=total[:], in_=rowsum[b][:], axis=mybir.AxisListType.X, op=ADD)
+                nm = keep.tile([P, 1], F32, name="negmean%d" % b)
+                nc.vector.tensor_scalar_mul(out=nm[:], in0=total[:], scalar1=-1.0 / H)
+                negmean.append(nm)
+                sq = keep.tile([P, 1], F32, name="sumsq%d" % b)
+                junk = junk_pool.tile([P, H], BF16, name="junk")
+                nc.scalar.activation(out=junk[:], in_=y[b][:], func=ACT.Square, bias=nm[:], scale=1.0, accum_out=sq[:])
+                sumsq.append(sq)
+                nc.vector.scalar_tensor_tensor(
+                    out=y[b][:], in0=y[b][:], scalar=nm[:], in1=g_all[:], op0=ADD, op1=MULT
+                )
+            if b >= 1:
+                a = b - 1
+                std = keep.tile([P, 1], F32, name="std%d" % a)
+                nc.scalar.activation(out=std[:], in_=sumsq[a][:], func=ACT.Sqrt, bias=LN_EPS, scale=1.0 / H)
+                rstd = keep.tile([P, 1], F32, name="rstd%d" % a)
+                nc.vector.reciprocal(out=rstd[:], in_=std[:])
+                nc.vector.scalar_tensor_tensor(
+                    out=y[a][:], in0=y[a][:], scalar=rstd[:], in1=b_all[:], op0=MULT, op1=ADD
+                )
+                nc.sync.dma_start(out=out[a], in_=y[a][:])

@@ -25,28 +25,10 @@ K_PASS = P * PACK
 PASSES = K // K_PASS
 WORDS_PASS = K_PASS // 2
 ROWS = 512
-BLOCKS = ROWS // P
 N_TILES = H // ROWS
+PAIRS = H // (2 * P)
 
 FLOPS = 2 * BATCH * P * K * H
-
-
-def quantise_rows(nc, psum_t, stage, ident, sources, codes, scales):
-    for g in range(PASSES):
-        grouped = stage.tile([P, ROWS * PACK], BF16, name="grouped", align_bytes=64)
-        grouped_words = grouped[:].bitcast(F32).rearrange("p (i r u) -> p i r u", i=BLOCKS, u=2)
-        for pair in range(BLOCKS // 2):
-            bank = psum_t.tile([P, 2, 2, P], F32, name="bank")
-            for i in range(2):
-                words = sources[2 * pair + i][:].bitcast(F32)
-                for u in range(2):
-                    first = WORDS_PASS * g + P * u
-                    nc.tensor.transpose(bank[:, i, u, :], words[:, first : first + P], ident[:])
-            nc.scalar.copy(
-                out=grouped_words[:, 2 * pair : 2 * pair + 2, :, :],
-                in_=bank[:].rearrange("p i u r -> p i r u"),
-            )
-        nc.vector.quantize_mx(out=codes[:, g, :].bitcast(FP8X4), scales=scales[:, g, :], in_=grouped[:])
 
 
 def tile_hierarchicalattention_pb_kernel(tc, ctx_heads, Wo, bo, features, ln_g, ln_b, out):
@@ -57,22 +39,27 @@ def tile_hierarchicalattention_pb_kernel(tc, ctx_heads, Wo, bo, features, ln_g, 
         stage = stack.enter_context(tc.tile_pool(name="stage", bufs=4))
         keep = stack.enter_context(tc.tile_pool(name="keep", bufs=1))
         junk_pool = stack.enter_context(tc.tile_pool(name="junk", bufs=2))
-        psum_t = stack.enter_context(tc.psum_pool(name="psum_t", bufs=4))
-        psum_acc = stack.enter_context(tc.psum_pool(name="psum_acc", bufs=4))
+        psum_vec = stack.enter_context(tc.psum_pool(name="psum_vec", bufs=3))
+        psum_work = stack.enter_context(tc.psum_pool(name="psum_work", bufs=5))
 
-        ident = const.tile([P, P], F32, name="ident")
-        make_identity(nc, ident[:])
-        ones = const.tile([P, P], BF16, name="ones")
-        nc.vector.memset(ones[:], 1.0)
-        vec_rows = const.tile([P, 3 * H], BF16, name="vec_rows")
-        nc.vector.memset(vec_rows[:].bitcast(I32), 0)
-        one_col = const.tile([P, 1], F32, name="one_col")
-        nc.vector.memset(one_col[:], 1.0)
-        warm = const.tile([P, 1], F32, name="warm")
-        nc.scalar.activation(out=warm[:], in_=one_col[:], func=ACT.Sqrt)
-
-        for v, vec in enumerate((bo, ln_g, ln_b)):
-            nc.sync.dma_start(out=vec_rows[0:1, v * H : (v + 1) * H], in_=vec.rearrange("(o n) -> o n", o=1))
+        vrow = []
+        for v in range(3):
+            t = const.tile([P, H], BF16, name="vrow%d" % v)
+            nc.vector.memset(t[:].bitcast(I32), 0)
+            vrow.append(t)
+        nc.sync.dma_start(out=vrow[0][0:1, :], in_=bo.rearrange("(o n) -> o n", o=1))
+        f_sb = []
+        for b in range(BATCH):
+            f = loads.tile([P, H], BF16, name="f_sb%d" % b)
+            nc.sync.dma_start(out=f[:], in_=features[b])
+            f_sb.append(f)
+        wo_sb = []
+        for r in range(H // P):
+            t = loads.tile([P, K], BF16, name="wo_sb%d" % r)
+            nc.sync.dma_start(out=t[:], in_=Wo[r * P : (r + 1) * P, :])
+            wo_sb.append(t)
+        nc.sync.dma_start(out=vrow[1][0:1, :], in_=ln_g.rearrange("(o n) -> o n", o=1))
+        nc.sync.dma_start(out=vrow[2][0:1, :], in_=ln_b.rearrange("(o n) -> o n", o=1))
         ctx_sb = []
         for b in range(BATCH):
             t = loads.tile([P, K], BF16, name="ctx_sb%d" % b)
@@ -80,56 +67,108 @@ def tile_hierarchicalattention_pb_kernel(tc, ctx_heads, Wo, bo, features, ln_g, 
                 out=t[:].rearrange("s (h d) -> s h d", h=HEADS), in_=ctx_heads[b].rearrange("h s d -> s h d")
             )
             ctx_sb.append(t)
-        wo_sb = []
-        f_sb = []
-        for r in range(H // P):
-            t = loads.tile([P, K], BF16, name="wo_sb%d" % r)
-            nc.sync.dma_start(out=t[:], in_=Wo[r * P : (r + 1) * P, :])
-            wo_sb.append(t)
-            if r == BLOCKS - 1:
-                for b in range(BATCH):
-                    f = loads.tile([P, H], BF16, name="f_sb%d" % b)
-                    nc.sync.dma_start(out=f[:], in_=features[b])
-                    f_sb.append(f)
 
-        spread = []
-        for v in range(3):
-            s = const.tile([P, H], BF16, name="spread%d" % v)
-            for j in range(N_TILES):
-                ps = psum_acc.tile([P, ROWS], F32, name="acc")
-                first = v * H + j * ROWS
-                nc.tensor.matmul(out=ps[:], lhsT=ones[:], rhs=vec_rows[:, first : first + ROWS], start=True, stop=True)
-                nc.vector.tensor_copy(out=s[:, j * ROWS : (j + 1) * ROWS], in_=ps[:])
-            spread.append(s)
-        bo_all, g_all, b_all = spread
+        ones = const.tile([P, P], BF16, name="ones")
+        nc.vector.memset(ones[:], 1.0)
+        ident = const.tile([P, P], F32, name="ident")
+        make_identity(nc, ident[:])
+        one_col = const.tile([P, 1], F32, name="one_col")
+        nc.vector.memset(one_col[:], 1.0)
+        warm = const.tile([P, 1], F32, name="warm")
+        nc.scalar.activation(out=warm[:], in_=one_col[:], func=ACT.Sqrt)
 
-        ctx_codes = keep.tile([P, PASSES, ROWS], U32, name="ctx_codes", align_bytes=64)
-        ctx_scales = keep.tile([P, PASSES, ROWS], U8, name="ctx_scales", align_bytes=64)
-        quantise_rows(nc, psum_t, stage, ident, ctx_sb, ctx_codes, ctx_scales)
+        def spread(pieces):
+            bank = psum_vec.tile([P, 2 * ROWS], BF16, name="vecbank")
+            for i, (v, first) in enumerate(pieces):
+                nc.tensor.matmul(
+                    out=bank[:, i * ROWS : (i + 1) * ROWS],
+                    lhsT=ones[:],
+                    rhs=vrow[v][:, first : first + ROWS],
+                    start=True,
+                    stop=True,
+                )
+            return bank
 
+        bo_a = spread([(0, 0), (0, ROWS)])
+        bo_b = spread([(0, 2 * ROWS)])
         y = []
         rowsum = []
         for b in range(BATCH):
-            y.append(keep.tile([P, H], F32, name="y%d" % b))
+            yt = keep.tile([P, H], F32, name="y%d" % b)
+            nc.vector.tensor_tensor(out=yt[:, 0 : 2 * ROWS], in0=f_sb[b][:, 0 : 2 * ROWS], in1=bo_a[:], op=ADD)
+            nc.vector.tensor_tensor(out=yt[:, 2 * ROWS : H], in0=f_sb[b][:, 2 * ROWS : H], in1=bo_b[:, 0:ROWS], op=ADD)
+            y.append(yt)
             rowsum.append(keep.tile([P, N_TILES], F32, name="rowsum%d" % b))
+
+        wo_codes = []
+        wo_scales = []
         for j in range(N_TILES):
-            wo_codes = keep.tile([P, PASSES, ROWS], U32, name="wo_codes%d" % j, align_bytes=64)
-            wo_scales = keep.tile([P, PASSES, ROWS], U8, name="wo_scales%d" % j, align_bytes=64)
-            quantise_rows(nc, psum_t, stage, ident, wo_sb[j * BLOCKS : (j + 1) * BLOCKS], wo_codes, wo_scales)
-            if j == 0:
-                for b in range(BATCH):
-                    nc.vector.tensor_tensor(out=y[b][:], in0=f_sb[b][:], in1=bo_all[:], op=ADD)
-            cols = slice(j * ROWS, (j + 1) * ROWS)
-            for b in range(BATCH):
-                tokens = slice(b * P, (b + 1) * P)
-                acc = psum_acc.tile([P, ROWS], F32, name="acc")
+            wo_codes.append(keep.tile([P, PASSES, ROWS], U32, name="wo_codes%d" % j, align_bytes=64))
+            wo_scales.append(keep.tile([P, PASSES, ROWS], U8, name="wo_scales%d" % j, align_bytes=64))
+        for pair in range(PAIRS):
+            j = pair // 2
+            cols = slice((pair % 2) * 2 * P, (pair % 2 + 1) * 2 * P)
+            for g in range(PASSES):
+                bank = psum_work.tile([P, 2, 2, P], F32, name="bank")
+                for i in range(2):
+                    words = wo_sb[2 * pair + i][:].bitcast(F32)
+                    for u in range(2):
+                        first = WORDS_PASS * g + P * u
+                        nc.tensor.transpose(bank[:, i, u, :], words[:, first : first + P], ident[:])
+                grouped = stage.tile([P, 2 * P * PACK], BF16, name="grouped", align_bytes=64)
+                nc.scalar.copy(
+                    out=grouped[:].bitcast(F32).rearrange("p (i r u) -> p i r u", i=2, u=2),
+                    in_=bank[:].rearrange("p i u r -> p i r u"),
+                )
+                nc.vector.quantize_mx(
+                    out=wo_codes[j][:, g, cols].bitcast(FP8X4), scales=wo_scales[j][:, g, cols], in_=grouped[:]
+                )
+
+        g_a = spread([(1, 0), (1, ROWS)])
+        gb = spread([(1, 2 * ROWS), (2, 0)])
+        b_b = spread([(2, ROWS), (2, 2 * ROWS)])
+
+        ctx_codes = []
+        ctx_scales = []
+        negmean = []
+        sumsq = []
+        normed = []
+
+        def prep_ctx(b):
+            codes = keep.tile([P, PASSES, P], U32, name="ctx_codes%d" % b, align_bytes=64)
+            scales = keep.tile([P, PASSES, P], U8, name="ctx_scales%d" % b, align_bytes=64)
+            words = ctx_sb[b][:].bitcast(F32)
+            grouped = stage.tile([P, PASSES * P * PACK], BF16, name="cgrouped", align_bytes=64)
+            gw = grouped[:].bitcast(F32).rearrange("p (g r u) -> p g r u", g=PASSES, u=2)
+            for g0, n in ((0, 2), (2, 1)):
+                bank = psum_work.tile([P, 2, 2, P], F32, name="bank")
+                for g in range(g0, g0 + n):
+                    for u in range(2):
+                        first = WORDS_PASS * g + P * u
+                        nc.tensor.transpose(bank[:, g - g0, u, :], words[:, first : first + P], ident[:])
+                nc.scalar.copy(
+                    out=gw[:, g0 : g0 + n, :, :], in_=bank[:, 0:n, :, :].rearrange("p g u r -> p g r u")
+                )
+            for g in range(PASSES):
+                nc.vector.quantize_mx(
+                    out=codes[:, g, :].bitcast(FP8X4),
+                    scales=scales[:, g, :],
+                    in_=grouped[:, g * P * PACK : (g + 1) * P * PACK],
+                )
+            ctx_codes.append(codes)
+            ctx_scales.append(scales)
+
+        def project(b):
+            for j in range(N_TILES):
+                cols = slice(j * ROWS, (j + 1) * ROWS)
+                acc = psum_work.tile([P, ROWS], F32, name="bank")
                 for g in range(PASSES):
                     nc.tensor.matmul_mx(
                         out=acc[:],
-                        lhsT=ctx_codes[:, g, tokens].bitcast(FP8X4),
-                        lhsT_scale=ctx_scales[:, g, tokens],
-                        rhs=wo_codes[:, g, :].bitcast(FP8X4),
-                        rhs_scale=wo_scales[:, g, :],
+                        lhsT=ctx_codes[b][:, g, :].bitcast(FP8X4),
+                        lhsT_scale=ctx_scales[b][:, g, :],
+                        rhs=wo_codes[j][:, g, :].bitcast(FP8X4),
+                        rhs_scale=wo_scales[j][:, g, :],
                         start=(g == 0),
                         stop=(g == PASSES - 1),
                     )
@@ -143,29 +182,45 @@ def tile_hierarchicalattention_pb_kernel(tc, ctx_heads, Wo, bo, features, ln_g, 
                     accum_out=rowsum[b][:, j : j + 1],
                 )
 
-        negmean = []
-        sumsq = []
-        for b in range(BATCH + 1):
-            if b < BATCH:
-                total = keep.tile([P, 1], F32, name="total%d" % b)
-                nc.vector.tensor_reduce(out=total[:], in_=rowsum[b][:], axis=mybir.AxisListType.X, op=ADD)
-                nm = keep.tile([P, 1], F32, name="negmean%d" % b)
-                nc.vector.tensor_scalar_mul(out=nm[:], in0=total[:], scalar1=-1.0 / H)
-                negmean.append(nm)
-                sq = keep.tile([P, 1], F32, name="sumsq%d" % b)
-                junk = junk_pool.tile([P, H], BF16, name="junk")
-                nc.scalar.activation(out=junk[:], in_=y[b][:], func=ACT.Square, bias=nm[:], scale=1.0, accum_out=sq[:])
-                sumsq.append(sq)
-                nc.vector.scalar_tensor_tensor(
-                    out=y[b][:], in0=y[b][:], scalar=nm[:], in1=g_all[:], op0=ADD, op1=MULT
-                )
-            if b >= 1:
-                a = b - 1
-                std = keep.tile([P, 1], F32, name="std%d" % a)
-                nc.scalar.activation(out=std[:], in_=sumsq[a][:], func=ACT.Sqrt, bias=LN_EPS, scale=1.0 / H)
-                rstd = keep.tile([P, 1], F32, name="rstd%d" % a)
-                nc.vector.reciprocal(out=rstd[:], in_=std[:])
-                nc.vector.scalar_tensor_tensor(
-                    out=y[a][:], in0=y[a][:], scalar=rstd[:], in1=b_all[:], op0=MULT, op1=ADD
-                )
-                nc.sync.dma_start(out=out[a], in_=y[a][:])
+        def centre(b):
+            total = keep.tile([P, 1], F32, name="total%d" % b)
+            nc.vector.tensor_reduce(out=total[:], in_=rowsum[b][:], axis=mybir.AxisListType.X, op=ADD)
+            nm = keep.tile([P, 1], F32, name="negmean%d" % b)
+            nc.vector.tensor_scalar_mul(out=nm[:], in0=total[:], scalar1=-1.0 / H)
+            sq = keep.tile([P, 1], F32, name="sumsq%d" % b)
+            junk = junk_pool.tile([P, H], BF16, name="junk")
+            nc.scalar.activation(out=junk[:], in_=y[b][:], func=ACT.Square, bias=nm[:], scale=1.0, accum_out=sq[:])
+            u = keep.tile([P, H], F32, name="normed%d" % b)
+            nc.vector.scalar_tensor_tensor(
+                out=u[:, 0 : 2 * ROWS], in0=y[b][:, 0 : 2 * ROWS], scalar=nm[:], in1=g_a[:], op0=ADD, op1=MULT
+            )
+            nc.vector.scalar_tensor_tensor(
+                out=u[:, 2 * ROWS : H], in0=y[b][:, 2 * ROWS : H], scalar=nm[:], in1=gb[:, 0:ROWS], op0=ADD, op1=MULT
+            )
+            negmean.append(nm)
+            sumsq.append(sq)
+            normed.append(u)
+
+        def finish(b):
+            std = keep.tile([P, 1], F32, name="std%d" % b)
+            nc.scalar.activation(out=std[:], in_=sumsq[b][:], func=ACT.Sqrt, bias=LN_EPS, scale=1.0 / H)
+            rstd = keep.tile([P, 1], F32, name="rstd%d" % b)
+            nc.vector.reciprocal(out=rstd[:], in_=std[:])
+            u = normed[b]
+            nc.vector.scalar_tensor_tensor(
+                out=u[:, 0:ROWS], in0=u[:, 0:ROWS], scalar=rstd[:], in1=gb[:, ROWS : 2 * ROWS], op0=MULT, op1=ADD
+            )
+            nc.sync.dma_start(out=out[b][:, 0:ROWS], in_=u[:, 0:ROWS])
+            nc.vector.scalar_tensor_tensor(
+                out=u[:, ROWS:H], in0=u[:, ROWS:H], scalar=rstd[:], in1=b_b[:], op0=MULT, op1=ADD
+            )
+            nc.sync.dma_start(out=out[b][:, ROWS:H], in_=u[:, ROWS:H])
+
+        for b in range(BATCH):
+            prep_ctx(b)
+        project(0)
+        for b in range(BATCH):
+            centre(b)
+            if b + 1 < BATCH:
+                project(b + 1)
+            finish(b)

@@ -27,6 +27,10 @@ WORDS_PASS = K_PASS // 2
 ROWS = 512
 N_TILES = H // ROWS
 PAIRS = H // (2 * P)
+EARLY = 0
+LAG = 1
+VCOLS = (768, 768, 768, 1536)
+GFIRST = 768
 
 FLOPS = 2 * BATCH * P * K * H
 
@@ -53,6 +57,17 @@ def tile_hierarchicalattention_pb_kernel(tc, ctx_heads, Wo, bo, features, ln_g, 
             f = loads.tile([P, H], BF16, name="f_sb%d" % b)
             nc.sync.dma_start(out=f[:], in_=features[b])
             f_sb.append(f)
+        ctx_sb = []
+
+        def load_ctx(b):
+            t = loads.tile([P, K], BF16, name="ctx_sb%d" % b)
+            nc.sync.dma_start(
+                out=t[:].rearrange("s (h d) -> s h d", h=HEADS), in_=ctx_heads[b].rearrange("h s d -> s h d")
+            )
+            ctx_sb.append(t)
+
+        for b in range(EARLY):
+            load_ctx(b)
         wo_sb = []
         for r in range(H // P):
             t = loads.tile([P, K], BF16, name="wo_sb%d" % r)
@@ -60,13 +75,8 @@ def tile_hierarchicalattention_pb_kernel(tc, ctx_heads, Wo, bo, features, ln_g, 
             wo_sb.append(t)
         nc.sync.dma_start(out=vrow[1][0:1, :], in_=ln_g.rearrange("(o n) -> o n", o=1))
         nc.sync.dma_start(out=vrow[2][0:1, :], in_=ln_b.rearrange("(o n) -> o n", o=1))
-        ctx_sb = []
-        for b in range(BATCH):
-            t = loads.tile([P, K], BF16, name="ctx_sb%d" % b)
-            nc.sync.dma_start(
-                out=t[:].rearrange("s (h d) -> s h d", h=HEADS), in_=ctx_heads[b].rearrange("h s d -> s h d")
-            )
-            ctx_sb.append(t)
+        for b in range(EARLY, BATCH):
+            load_ctx(b)
 
         ones = const.tile([P, P], BF16, name="ones")
         nc.vector.memset(ones[:], 1.0)
@@ -100,34 +110,6 @@ def tile_hierarchicalattention_pb_kernel(tc, ctx_heads, Wo, bo, features, ln_g, 
             y.append(yt)
             rowsum.append(keep.tile([P, N_TILES], F32, name="rowsum%d" % b))
 
-        wo_codes = []
-        wo_scales = []
-        for j in range(N_TILES):
-            wo_codes.append(keep.tile([P, PASSES, ROWS], U32, name="wo_codes%d" % j, align_bytes=64))
-            wo_scales.append(keep.tile([P, PASSES, ROWS], U8, name="wo_scales%d" % j, align_bytes=64))
-        for pair in range(PAIRS):
-            j = pair // 2
-            cols = slice((pair % 2) * 2 * P, (pair % 2 + 1) * 2 * P)
-            for g in range(PASSES):
-                bank = psum_work.tile([P, 2, 2, P], F32, name="bank")
-                for i in range(2):
-                    words = wo_sb[2 * pair + i][:].bitcast(F32)
-                    for u in range(2):
-                        first = WORDS_PASS * g + P * u
-                        nc.tensor.transpose(bank[:, i, u, :], words[:, first : first + P], ident[:])
-                grouped = stage.tile([P, 2 * P * PACK], BF16, name="grouped", align_bytes=64)
-                nc.scalar.copy(
-                    out=grouped[:].bitcast(F32).rearrange("p (i r u) -> p i r u", i=2, u=2),
-                    in_=bank[:].rearrange("p i u r -> p i r u"),
-                )
-                nc.vector.quantize_mx(
-                    out=wo_codes[j][:, g, cols].bitcast(FP8X4), scales=wo_scales[j][:, g, cols], in_=grouped[:]
-                )
-
-        g_a = spread([(1, 0), (1, ROWS)])
-        gb = spread([(1, 2 * ROWS), (2, 0)])
-        b_b = spread([(2, ROWS), (2, 2 * ROWS)])
-
         ctx_codes = []
         ctx_scales = []
         negmean = []
@@ -158,8 +140,8 @@ def tile_hierarchicalattention_pb_kernel(tc, ctx_heads, Wo, bo, features, ln_g, 
             ctx_codes.append(codes)
             ctx_scales.append(scales)
 
-        def project(b):
-            for j in range(N_TILES):
+        def project(b, chunks):
+            for j in chunks:
                 cols = slice(j * ROWS, (j + 1) * ROWS)
                 acc = psum_work.tile([P, ROWS], F32, name="bank")
                 for g in range(PASSES):
@@ -182,45 +164,110 @@ def tile_hierarchicalattention_pb_kernel(tc, ctx_heads, Wo, bo, features, ln_g, 
                     accum_out=rowsum[b][:, j : j + 1],
                 )
 
+        wo_codes = []
+        wo_scales = []
+        for j in range(N_TILES):
+            wo_codes.append(keep.tile([P, PASSES, ROWS], U32, name="wo_codes%d" % j, align_bytes=64))
+            wo_scales.append(keep.tile([P, PASSES, ROWS], U8, name="wo_scales%d" % j, align_bytes=64))
+        for b in range(EARLY):
+            prep_ctx(b)
+        for pair in range(PAIRS):
+            j = pair // 2
+            cols = slice((pair % 2) * 2 * P, (pair % 2 + 1) * 2 * P)
+            for g in range(PASSES):
+                bank = psum_work.tile([P, 2, 2, P], F32, name="bank")
+                for i in range(2):
+                    words = wo_sb[2 * pair + i][:].bitcast(F32)
+                    for u in range(2):
+                        first = WORDS_PASS * g + P * u
+                        nc.tensor.transpose(bank[:, i, u, :], words[:, first : first + P], ident[:])
+                grouped = stage.tile([P, 2 * P * PACK], BF16, name="grouped", align_bytes=64)
+                nc.scalar.copy(
+                    out=grouped[:].bitcast(F32).rearrange("p (i r u) -> p i r u", i=2, u=2),
+                    in_=bank[:].rearrange("p i u r -> p i r u"),
+                )
+                nc.vector.quantize_mx(
+                    out=wo_codes[j][:, g, cols].bitcast(FP8X4), scales=wo_scales[j][:, g, cols], in_=grouped[:]
+                )
+            if pair % 2 == 1 and j >= LAG:
+                for b in range(EARLY):
+                    project(b, [j - LAG])
+        for jj in range(N_TILES - LAG, N_TILES):
+            for b in range(EARLY):
+                project(b, [jj])
+
+        tail_bank = spread([(1, 2 * ROWS), (2, 2 * ROWS)])
+        g_bank = spread([(1, 0), (1, ROWS)])
+        b_bank = spread([(2, 0), (2, ROWS)])
+        g_sb = const.tile([P, H - GFIRST], BF16, name="g_sb")
+        b_sb = const.tile([P, H - GFIRST], BF16, name="b_sb")
+        nc.scalar.copy(out=g_sb[:, 2 * ROWS - GFIRST :], in_=tail_bank[:, 0:ROWS])
+        nc.scalar.copy(out=b_sb[:, 2 * ROWS - GFIRST :], in_=tail_bank[:, ROWS : 2 * ROWS])
+        nc.scalar.copy(out=g_sb[:, 0 : 2 * ROWS - GFIRST], in_=g_bank[:, GFIRST : 2 * ROWS])
+        nc.scalar.copy(out=b_sb[:, 0 : 2 * ROWS - GFIRST], in_=b_bank[:, GFIRST : 2 * ROWS])
+
+        rstds = []
+
+        def vector_pieces(b):
+            cv = VCOLS[b]
+            pieces = [(0, min(cv, 2 * ROWS), g_bank, b_bank, 0, 0)]
+            if cv > 2 * ROWS:
+                pieces.append((2 * ROWS, cv, tail_bank, tail_bank, 0, ROWS))
+            return pieces
+
         def centre(b):
-            total = keep.tile([P, 1], F32, name="total%d" % b)
-            nc.vector.tensor_reduce(out=total[:], in_=rowsum[b][:], axis=mybir.AxisListType.X, op=ADD)
             nm = keep.tile([P, 1], F32, name="negmean%d" % b)
-            nc.vector.tensor_scalar_mul(out=nm[:], in0=total[:], scalar1=-1.0 / H)
+            junk3 = keep.tile([P, N_TILES], F32, name="junk3_%d" % b)
+            nc.scalar.activation(out=junk3[:], in_=rowsum[b][:], func=ACT.Identity, scale=-1.0 / H, accum_out=nm[:])
             sq = keep.tile([P, 1], F32, name="sumsq%d" % b)
             junk = junk_pool.tile([P, H], BF16, name="junk")
             nc.scalar.activation(out=junk[:], in_=y[b][:], func=ACT.Square, bias=nm[:], scale=1.0, accum_out=sq[:])
             u = keep.tile([P, H], F32, name="normed%d" % b)
-            nc.vector.scalar_tensor_tensor(
-                out=u[:, 0 : 2 * ROWS], in0=y[b][:, 0 : 2 * ROWS], scalar=nm[:], in1=g_a[:], op0=ADD, op1=MULT
-            )
-            nc.vector.scalar_tensor_tensor(
-                out=u[:, 2 * ROWS : H], in0=y[b][:, 2 * ROWS : H], scalar=nm[:], in1=gb[:, 0:ROWS], op0=ADD, op1=MULT
-            )
+            for lo, hi, gbank, bbank, goff, boff in vector_pieces(b):
+                nc.vector.scalar_tensor_tensor(
+                    out=u[:, lo:hi], in0=y[b][:, lo:hi], scalar=nm[:], in1=gbank[:, goff : goff + hi - lo], op0=ADD, op1=MULT
+                )
             negmean.append(nm)
             sumsq.append(sq)
             normed.append(u)
 
-        def finish(b):
+        def scale(b):
             std = keep.tile([P, 1], F32, name="std%d" % b)
             nc.scalar.activation(out=std[:], in_=sumsq[b][:], func=ACT.Sqrt, bias=LN_EPS, scale=1.0 / H)
             rstd = keep.tile([P, 1], F32, name="rstd%d" % b)
             nc.vector.reciprocal(out=rstd[:], in_=std[:])
+            rstds.append(rstd)
+            cv = VCOLS[b]
+            if cv < H:
+                u = normed[b]
+                shift = keep.tile([P, 1], F32, name="shift%d" % b)
+                nc.scalar.activation(out=shift[:], in_=negmean[b][:], func=ACT.Copy, scale=rstd[:])
+                unit = stage.tile([P, H - GFIRST], F32, name="unit")
+                nc.scalar.activation(
+                    out=unit[:, 0 : H - cv], in_=y[b][:, cv:H], func=ACT.Identity, scale=rstd[:], bias=shift[:]
+                )
+                scaled = stage.tile([P, H - GFIRST], F32, name="scaled")
+                nc.gpsimd.tensor_tensor(
+                    out=scaled[:, 0 : H - cv], in0=unit[:, 0 : H - cv], in1=g_sb[:, cv - GFIRST :], op=MULT
+                )
+                nc.gpsimd.tensor_tensor(out=u[:, cv:H], in0=scaled[:, 0 : H - cv], in1=b_sb[:, cv - GFIRST :], op=ADD)
+
+        def finish(b):
             u = normed[b]
-            nc.vector.scalar_tensor_tensor(
-                out=u[:, 0:ROWS], in0=u[:, 0:ROWS], scalar=rstd[:], in1=gb[:, ROWS : 2 * ROWS], op0=MULT, op1=ADD
-            )
-            nc.sync.dma_start(out=out[b][:, 0:ROWS], in_=u[:, 0:ROWS])
-            nc.vector.scalar_tensor_tensor(
-                out=u[:, ROWS:H], in0=u[:, ROWS:H], scalar=rstd[:], in1=b_b[:], op0=MULT, op1=ADD
-            )
-            nc.sync.dma_start(out=out[b][:, ROWS:H], in_=u[:, ROWS:H])
+            for lo, hi, gbank, bbank, goff, boff in vector_pieces(b):
+                nc.vector.scalar_tensor_tensor(
+                    out=u[:, lo:hi], in0=u[:, lo:hi], scalar=rstds[b][:], in1=bbank[:, boff : boff + hi - lo], op0=MULT, op1=ADD
+                )
+                nc.sync.dma_start(out=out[b][:, lo:hi], in_=u[:, lo:hi])
+            if VCOLS[b] < H:
+                nc.sync.dma_start(out=out[b][:, VCOLS[b] : H], in_=u[:, VCOLS[b] : H])
 
         for b in range(BATCH):
             prep_ctx(b)
-        project(0)
+        project(0, range(N_TILES))
         for b in range(BATCH):
             centre(b)
+            scale(b)
             if b + 1 < BATCH:
-                project(b + 1)
+                project(b + 1, range(N_TILES))
             finish(b)

@@ -27,7 +27,7 @@ WORDS_PASS = K_PASS // 2
 ROWS = 512
 N_TILES = H // ROWS
 PAIRS = H // (2 * P)
-EARLY = 0
+EARLY = 1
 LAG = 1
 VCOLS = (768, 768, 768, 1536)
 GFIRST = 768
@@ -52,6 +52,8 @@ def tile_hierarchicalattention_pb_kernel(tc, ctx_heads, Wo, bo, features, ln_g, 
             nc.vector.memset(t[:].bitcast(I32), 0)
             vrow.append(t)
         nc.sync.dma_start(out=vrow[0][0:1, :], in_=bo.rearrange("(o n) -> o n", o=1))
+        nc.scalar.dma_start(out=vrow[1][0:1, :], in_=ln_g.rearrange("(o n) -> o n", o=1))
+        nc.scalar.dma_start(out=vrow[2][0:1, :], in_=ln_b.rearrange("(o n) -> o n", o=1))
         f_sb = []
         for b in range(BATCH):
             f = loads.tile([P, H], BF16, name="f_sb%d" % b)
@@ -73,8 +75,6 @@ def tile_hierarchicalattention_pb_kernel(tc, ctx_heads, Wo, bo, features, ln_g, 
             t = loads.tile([P, K], BF16, name="wo_sb%d" % r)
             nc.sync.dma_start(out=t[:], in_=Wo[r * P : (r + 1) * P, :])
             wo_sb.append(t)
-        nc.sync.dma_start(out=vrow[1][0:1, :], in_=ln_g.rearrange("(o n) -> o n", o=1))
-        nc.sync.dma_start(out=vrow[2][0:1, :], in_=ln_b.rearrange("(o n) -> o n", o=1))
         for b in range(EARLY, BATCH):
             load_ctx(b)
 
@@ -103,10 +103,22 @@ def tile_hierarchicalattention_pb_kernel(tc, ctx_heads, Wo, bo, features, ln_g, 
         bo_b = spread([(0, 2 * ROWS)])
         y = []
         rowsum = []
+        bo_sb = const.tile([P, H], BF16, name="bo_sb")
+        nc.scalar.copy(out=bo_sb[:, 0 : 2 * ROWS], in_=bo_a[:])
+        nc.scalar.copy(out=bo_sb[:, 2 * ROWS : H], in_=bo_b[:, 0:ROWS])
+        tail_bank = spread([(1, 2 * ROWS), (2, 2 * ROWS)])
+        g_bank = spread([(1, 0), (1, ROWS)])
+        b_bank = spread([(2, 0), (2, ROWS)])
+        g_sb = const.tile([P, H - GFIRST], BF16, name="g_sb")
+        b_sb = const.tile([P, H - GFIRST], BF16, name="b_sb")
+        nc.scalar.copy(out=g_sb[:, 2 * ROWS - GFIRST :], in_=tail_bank[:, 0:ROWS])
+        nc.scalar.copy(out=b_sb[:, 2 * ROWS - GFIRST :], in_=tail_bank[:, ROWS : 2 * ROWS])
+        nc.scalar.copy(out=g_sb[:, 0 : 2 * ROWS - GFIRST], in_=g_bank[:, GFIRST : 2 * ROWS])
+        nc.scalar.copy(out=b_sb[:, 0 : 2 * ROWS - GFIRST], in_=b_bank[:, GFIRST : 2 * ROWS])
+
         for b in range(BATCH):
             yt = keep.tile([P, H], F32, name="y%d" % b)
-            nc.vector.tensor_tensor(out=yt[:, 0 : 2 * ROWS], in0=f_sb[b][:, 0 : 2 * ROWS], in1=bo_a[:], op=ADD)
-            nc.vector.tensor_tensor(out=yt[:, 2 * ROWS : H], in0=f_sb[b][:, 2 * ROWS : H], in1=bo_b[:, 0:ROWS], op=ADD)
+            nc.vector.tensor_tensor(out=yt[:], in0=f_sb[b][:], in1=bo_sb[:], op=ADD)
             y.append(yt)
             rowsum.append(keep.tile([P, N_TILES], F32, name="rowsum%d" % b))
 
@@ -196,16 +208,6 @@ def tile_hierarchicalattention_pb_kernel(tc, ctx_heads, Wo, bo, features, ln_g, 
             for b in range(EARLY):
                 project(b, [jj])
 
-        tail_bank = spread([(1, 2 * ROWS), (2, 2 * ROWS)])
-        g_bank = spread([(1, 0), (1, ROWS)])
-        b_bank = spread([(2, 0), (2, ROWS)])
-        g_sb = const.tile([P, H - GFIRST], BF16, name="g_sb")
-        b_sb = const.tile([P, H - GFIRST], BF16, name="b_sb")
-        nc.scalar.copy(out=g_sb[:, 2 * ROWS - GFIRST :], in_=tail_bank[:, 0:ROWS])
-        nc.scalar.copy(out=b_sb[:, 2 * ROWS - GFIRST :], in_=tail_bank[:, ROWS : 2 * ROWS])
-        nc.scalar.copy(out=g_sb[:, 0 : 2 * ROWS - GFIRST], in_=g_bank[:, GFIRST : 2 * ROWS])
-        nc.scalar.copy(out=b_sb[:, 0 : 2 * ROWS - GFIRST], in_=b_bank[:, GFIRST : 2 * ROWS])
-
         rstds = []
 
         def vector_pieces(b):
@@ -262,12 +264,13 @@ def tile_hierarchicalattention_pb_kernel(tc, ctx_heads, Wo, bo, features, ln_g, 
             if VCOLS[b] < H:
                 nc.sync.dma_start(out=out[b][:, VCOLS[b] : H], in_=u[:, VCOLS[b] : H])
 
-        for b in range(BATCH):
+        for b in range(EARLY, BATCH):
             prep_ctx(b)
-        project(0, range(N_TILES))
+        if EARLY == 0:
+            project(0, range(N_TILES))
         for b in range(BATCH):
             centre(b)
             scale(b)
-            if b + 1 < BATCH:
+            if max(EARLY, 1) <= b + 1 < BATCH:
                 project(b + 1, range(N_TILES))
             finish(b)

@@ -29,8 +29,8 @@ N_TILES = H // ROWS
 PAIRS = H // (2 * P)
 EARLY = 1
 LAG = 1
-VCOLS = (768, 768, 768, 1536)
-GFIRST = 768
+VCOLS = (512, 640, 1152, 1536)
+GFIRST = 512
 
 FLOPS = 2 * BATCH * P * K * H
 

from contextlib import ExitStack

import concourse.mybir as mybir
from concourse.masks import make_identity

FP8X4 = mybir.dt.float8_e4m3fn_x4
BF16 = mybir.dt.bfloat16
F32 = mybir.dt.float32
I32 = mybir.dt.int32
U32 = mybir.dt.uint32
U8 = mybir.dt.uint8
ADD = mybir.AluOpType.add
MULT = mybir.AluOpType.mult
ACT = mybir.ActivationFunctionType

P = 128
BATCH = 4
HEADS = 12
K = 1536
H = 1536
LN_EPS = 1e-5

PACK = 4
K_PASS = P * PACK
PASSES = K // K_PASS
WORDS_PASS = K_PASS // 2
ROWS = 512
N_TILES = H // ROWS
PAIRS = H // (2 * P)
EARLY = 1
LAG = 1
VCOLS = (512, 640, 1152, 1536)
GFIRST = 512

FLOPS = 2 * BATCH * P * K * H


def tile_hierarchicalattention_pb_kernel(tc, ctx_heads, Wo, bo, features, ln_g, ln_b, out):
    nc = tc.nc
    with ExitStack() as stack:
        const = stack.enter_context(tc.tile_pool(name="const", bufs=1))
        loads = stack.enter_context(tc.tile_pool(name="loads", bufs=1))
        stage = stack.enter_context(tc.tile_pool(name="stage", bufs=4))
        keep = stack.enter_context(tc.tile_pool(name="keep", bufs=1))
        junk_pool = stack.enter_context(tc.tile_pool(name="junk", bufs=2))
        psum_vec = stack.enter_context(tc.psum_pool(name="psum_vec", bufs=3))
        psum_work = stack.enter_context(tc.psum_pool(name="psum_work", bufs=5))

        vrow = []
        for v in range(3):
            t = const.tile([P, H], BF16, name="vrow%d" % v)
            nc.vector.memset(t[:].bitcast(I32), 0)
            vrow.append(t)
        nc.sync.dma_start(out=vrow[0][0:1, :], in_=bo.rearrange("(o n) -> o n", o=1))
        nc.scalar.dma_start(out=vrow[1][0:1, :], in_=ln_g.rearrange("(o n) -> o n", o=1))
        nc.scalar.dma_start(out=vrow[2][0:1, :], in_=ln_b.rearrange("(o n) -> o n", o=1))
        f_sb = []
        for b in range(BATCH):
            f = loads.tile([P, H], BF16, name="f_sb%d" % b)
            nc.sync.dma_start(out=f[:], in_=features[b])
            f_sb.append(f)
        ctx_sb = []

        def load_ctx(b):
            t = loads.tile([P, K], BF16, name="ctx_sb%d" % b)
            nc.sync.dma_start(
                out=t[:].rearrange("s (h d) -> s h d", h=HEADS), in_=ctx_heads[b].rearrange("h s d -> s h d")
            )
            ctx_sb.append(t)

        for b in range(EARLY):
            load_ctx(b)
        wo_sb = []
        for r in range(H // P):
            t = loads.tile([P, K], BF16, name="wo_sb%d" % r)
            nc.sync.dma_start(out=t[:], in_=Wo[r * P : (r + 1) * P, :])
            wo_sb.append(t)
        for b in range(EARLY, BATCH):
            load_ctx(b)

        ones = const.tile([P, P], BF16, name="ones")
        nc.vector.memset(ones[:], 1.0)
        ident = const.tile([P, P], F32, name="ident")
        make_identity(nc, ident[:])
        one_col = const.tile([P, 1], F32, name="one_col")
        nc.vector.memset(one_col[:], 1.0)
        warm = const.tile([P, 1], F32, name="warm")
        nc.scalar.activation(out=warm[:], in_=one_col[:], func=ACT.Sqrt)

        def spread(pieces):
            bank = psum_vec.tile([P, 2 * ROWS], BF16, name="vecbank")
            for i, (v, first) in enumerate(pieces):
                nc.tensor.matmul(
                    out=bank[:, i * ROWS : (i + 1) * ROWS],
                    lhsT=ones[:],
                    rhs=vrow[v][:, first : first + ROWS],
                    start=True,
                    stop=True,
                )
            return bank

        bo_a = spread([(0, 0), (0, ROWS)])
        bo_b = spread([(0, 2 * ROWS)])
        y = []
        rowsum = []
        bo_sb = const.tile([P, H], BF16, name="bo_sb")
        nc.scalar.copy(out=bo_sb[:, 0 : 2 * ROWS], in_=bo_a[:])
        nc.scalar.copy(out=bo_sb[:, 2 * ROWS : H], in_=bo_b[:, 0:ROWS])
        tail_bank = spread([(1, 2 * ROWS), (2, 2 * ROWS)])
        g_bank = spread([(1, 0), (1, ROWS)])
        b_bank = spread([(2, 0), (2, ROWS)])
        g_sb = const.tile([P, H - GFIRST], BF16, name="g_sb")
        b_sb = const.tile([P, H - GFIRST], BF16, name="b_sb")
        nc.scalar.copy(out=g_sb[:, 2 * ROWS - GFIRST :], in_=tail_bank[:, 0:ROWS])
        nc.scalar.copy(out=b_sb[:, 2 * ROWS - GFIRST :], in_=tail_bank[:, ROWS : 2 * ROWS])
        nc.scalar.copy(out=g_sb[:, 0 : 2 * ROWS - GFIRST], in_=g_bank[:, GFIRST : 2 * ROWS])
        nc.scalar.copy(out=b_sb[:, 0 : 2 * ROWS - GFIRST], in_=b_bank[:, GFIRST : 2 * ROWS])

        for b in range(BATCH):
            yt = keep.tile([P, H], F32, name="y%d" % b)
            nc.vector.tensor_tensor(out=yt[:], in0=f_sb[b][:], in1=bo_sb[:], op=ADD)
            y.append(yt)
            rowsum.append(keep.tile([P, N_TILES], F32, name="rowsum%d" % b))

        ctx_codes = []
        ctx_scales = []
        negmean = []
        sumsq = []
        normed = []

        def prep_ctx(b):
            codes = keep.tile([P, PASSES, P], U32, name="ctx_codes%d" % b, align_bytes=64)
            scales = keep.tile([P, PASSES, P], U8, name="ctx_scales%d" % b, align_bytes=64)
            words = ctx_sb[b][:].bitcast(F32)
            grouped = stage.tile([P, PASSES * P * PACK], BF16, name="cgrouped", align_bytes=64)
            gw = grouped[:].bitcast(F32).rearrange("p (g r u) -> p g r u", g=PASSES, u=2)
            for g0, n in ((0, 2), (2, 1)):
                bank = psum_work.tile([P, 2, 2, P], F32, name="bank")
                for g in range(g0, g0 + n):
                    for u in range(2):
                        first = WORDS_PASS * g + P * u
                        nc.tensor.transpose(bank[:, g - g0, u, :], words[:, first : first + P], ident[:])
                nc.scalar.copy(
                    out=gw[:, g0 : g0 + n, :, :], in_=bank[:, 0:n, :, :].rearrange("p g u r -> p g r u")
                )
            for g in range(PASSES):
                nc.vector.quantize_mx(
                    out=codes[:, g, :].bitcast(FP8X4),
                    scales=scales[:, g, :],
                    in_=grouped[:, g * P * PACK : (g + 1) * P * PACK],
                )
            ctx_codes.append(codes)
            ctx_scales.append(scales)

        def project(b, chunks):
            for j in chunks:
                cols = slice(j * ROWS, (j + 1) * ROWS)
                acc = psum_work.tile([P, ROWS], F32, name="bank")
                for g in range(PASSES):
                    nc.tensor.matmul_mx(
                        out=acc[:],
                        lhsT=ctx_codes[b][:, g, :].bitcast(FP8X4),
                        lhsT_scale=ctx_scales[b][:, g, :],
                        rhs=wo_codes[j][:, g, :].bitcast(FP8X4),
                        rhs_scale=wo_scales[j][:, g, :],
                        start=(g == 0),
                        stop=(g == PASSES - 1),
                    )
                nc.vector.scalar_tensor_tensor(
                    out=y[b][:, cols],
                    in0=acc[:],
                    scalar=1.0,
                    in1=y[b][:, cols],
                    op0=MULT,
                    op1=ADD,
                    accum_out=rowsum[b][:, j : j + 1],
                )

        wo_codes = []
        wo_scales = []
        for j in range(N_TILES):
            wo_codes.append(keep.tile([P, PASSES, ROWS], U32, name="wo_codes%d" % j, align_bytes=64))
            wo_scales.append(keep.tile([P, PASSES, ROWS], U8, name="wo_scales%d" % j, align_bytes=64))
        for b in range(EARLY):
            prep_ctx(b)
        for pair in range(PAIRS):
            j = pair // 2
            cols = slice((pair % 2) * 2 * P, (pair % 2 + 1) * 2 * P)
            for g in range(PASSES):
                bank = psum_work.tile([P, 2, 2, P], F32, name="bank")
                for i in range(2):
                    words = wo_sb[2 * pair + i][:].bitcast(F32)
                    for u in range(2):
                        first = WORDS_PASS * g + P * u
                        nc.tensor.transpose(bank[:, i, u, :], words[:, first : first + P], ident[:])
                grouped = stage.tile([P, 2 * P * PACK], BF16, name="grouped", align_bytes=64)
                nc.scalar.copy(
                    out=grouped[:].bitcast(F32).rearrange("p (i r u) -> p i r u", i=2, u=2),
                    in_=bank[:].rearrange("p i u r -> p i r u"),
                )
                nc.vector.quantize_mx(
                    out=wo_codes[j][:, g, cols].bitcast(FP8X4), scales=wo_scales[j][:, g, cols], in_=grouped[:]
                )
            if pair % 2 == 1 and j >= LAG:
                for b in range(EARLY):
                    project(b, [j - LAG])
        for jj in range(N_TILES - LAG, N_TILES):
            for b in range(EARLY):
                project(b, [jj])

        rstds = []

        def vector_pieces(b):
            cv = VCOLS[b]
            pieces = [(0, min(cv, 2 * ROWS), g_bank, b_bank, 0, 0)]
            if cv > 2 * ROWS:
                pieces.append((2 * ROWS, cv, tail_bank, tail_bank, 0, ROWS))
            return pieces

        def centre(b):
            nm = keep.tile([P, 1], F32, name="negmean%d" % b)
            junk3 = keep.tile([P, N_TILES], F32, name="junk3_%d" % b)
            nc.scalar.activation(out=junk3[:], in_=rowsum[b][:], func=ACT.Identity, scale=-1.0 / H, accum_out=nm[:])
            sq = keep.tile([P, 1], F32, name="sumsq%d" % b)
            junk = junk_pool.tile([P, H], BF16, name="junk")
            nc.scalar.activation(out=junk[:], in_=y[b][:], func=ACT.Square, bias=nm[:], scale=1.0, accum_out=sq[:])
            u = keep.tile([P, H], F32, name="normed%d" % b)
            for lo, hi, gbank, bbank, goff, boff in vector_pieces(b):
                nc.vector.scalar_tensor_tensor(
                    out=u[:, lo:hi], in0=y[b][:, lo:hi], scalar=nm[:], in1=gbank[:, goff : goff + hi - lo], op0=ADD, op1=MULT
                )
            negmean.append(nm)
            sumsq.append(sq)
            normed.append(u)

        def scale(b):
            std = keep.tile([P, 1], F32, name="std%d" % b)
            nc.scalar.activation(out=std[:], in_=sumsq[b][:], func=ACT.Sqrt, bias=LN_EPS, scale=1.0 / H)
            rstd = keep.tile([P, 1], F32, name="rstd%d" % b)
            nc.vector.reciprocal(out=rstd[:], in_=std[:])
            rstds.append(rstd)
            cv = VCOLS[b]
            if cv < H:
                u = normed[b]
                shift = keep.tile([P, 1], F32, name="shift%d" % b)
                nc.scalar.activation(out=shift[:], in_=negmean[b][:], func=ACT.Copy, scale=rstd[:])
                unit = stage.tile([P, H - GFIRST], F32, name="unit")
                nc.scalar.activation(
                    out=unit[:, 0 : H - cv], in_=y[b][:, cv:H], func=ACT.Identity, scale=rstd[:], bias=shift[:]
                )
                scaled = stage.tile([P, H - GFIRST], F32, name="scaled")
                nc.gpsimd.tensor_tensor(
                    out=scaled[:, 0 : H - cv], in0=unit[:, 0 : H - cv], in1=g_sb[:, cv - GFIRST :], op=MULT
                )
                nc.gpsimd.tensor_tensor(out=u[:, cv:H], in0=scaled[:, 0 : H - cv], in1=b_sb[:, cv - GFIRST :], op=ADD)

        def finish(b):
            u = normed[b]
            for lo, hi, gbank, bbank, goff, boff in vector_pieces(b):
                nc.vector.scalar_tensor_tensor(
                    out=u[:, lo:hi], in0=u[:, lo:hi], scalar=rstds[b][:], in1=bbank[:, boff : boff + hi - lo], op0=MULT, op1=ADD
                )
                nc.sync.dma_start(out=out[b][:, lo:hi], in_=u[:, lo:hi])
            if VCOLS[b] < H:
                nc.sync.dma_start(out=out[b][:, VCOLS[b] : H], in_=u[:, VCOLS[b] : H])

        for b in range(EARLY, BATCH):
            prep_ctx(b)
        if EARLY == 0:
            project(0, range(N_TILES))
        for b in range(BATCH):
            centre(b)
            scale(b)
            if max(EARLY, 1) <= b + 1 < BATCH:
                project(b + 1, range(N_TILES))
            finish(b)
